import numpy as np
import ml_dtypes


def mxq(x, axis, fmt="e4m3"):
    dtype, down = {"e4m3": (ml_dtypes.float8_e4m3fn, 7), "e5m2": (ml_dtypes.float8_e5m2, 14)}[fmt]
    v = np.moveaxis(np.asarray(x, np.float32).astype(ml_dtypes.bfloat16).astype(np.float64), axis, -1)
    blocks = v.reshape(v.shape[:-1] + (-1, 32))
    amax = np.abs(blocks).max(-1, keepdims=True)
    byte = np.maximum(np.where(amax > 0, np.frexp(amax)[1] - 1 + 127, 0) - down, 1)
    scale = np.exp2(byte - 127.0)
    codes = (blocks / scale).astype(np.float32).astype(dtype).astype(np.float64)
    return np.moveaxis((codes * scale).reshape(v.shape), -1, axis)


WIDE = False


def mx_kscale(k):
    if not WIDE:
        return np.ones(k)
    levels = np.array([10, -10, 5, -5, 0])
    a = np.random.permutation(np.resize(levels, k // 512 * 4)).reshape(k // 512, 4)
    idx = np.arange(k)
    return np.exp2(a[idx // 512, idx % 128 // 32])


BF16 = ml_dtypes.bfloat16


def bf(x):
    return np.asarray(x, np.float32).astype(BF16)


def f64(x):
    return np.asarray(x).astype(np.float64)


B, G, C, F, NC = 128, 3, 512, 8192, 4096
HW = G * G
P_GEM = 3.0
EPS_GEM = 1e-6
EPS_NORM = 1e-12


def l2n(v, axis):
    n = np.sqrt(np.sum(v * v, axis=axis, keepdims=True))
    return v / np.maximum(n, EPS_NORM)


def setup_inputs():
    s, t = mx_kscale(F), mx_kscale(C)
    z = np.random.standard_normal((B, HW, F))
    return {"hdn": bf(z / (1.0 + np.exp(-1.702 * z)) * s),
            "fc2_w": bf(np.random.standard_normal((F, C)) * 1.5 / np.sqrt(F) / s[:, None] * t),
            "fc2_b": bf(np.random.standard_normal(C) * 0.3 * t),
            "head_w": bf(np.random.standard_normal((C, NC)) / np.sqrt(C) / t[:, None]),
            "head_b": bf(np.random.standard_normal(NC) * 0.3)}


def reference(hdn, fc2_w, fc2_b, head_w, head_b):
    tok = (mxq(f64(hdn), 2, "e4m3") @ mxq(f64(fc2_w), 0, "e4m3")) + f64(fc2_b)
    g = np.mean(np.maximum(tok, EPS_GEM) ** P_GEM, axis=1) ** (1.0 / P_GEM)
    desc = (mxq(g, 1, "e4m3") @ mxq(f64(head_w), 0, "e4m3")) + f64(head_b)
    return l2n(desc, 1)

@@ -1,0 +1,342 @@
+from contextlib import ExitStack
+
+import concourse.mybir as mybir
+from concourse.masks import make_identity
+
+F32 = mybir.dt.float32
+BF16 = mybir.dt.bfloat16
+U32 = mybir.dt.uint32
+U8 = mybir.dt.uint8
+FP8X4 = mybir.dt.float8_e4m3fn_x4
+ALU = mybir.AluOpType
+ACT = mybir.ActivationFunctionType
+AX = mybir.AxisListType
+
+P = 128
+PACK = 4
+K_PASS = P * PACK
+TOKENS = 9
+HIDDEN = 8192
+CHANNELS = 512
+CLASSES = 4096
+PASSES = HIDDEN // K_PASS
+C_TILES = CHANNELS // P
+BANK = 512
+D_BANKS = CLASSES // BANK
+
+EPS_GEM = 1e-6
+EPS_NORM = 1e-12
+
+FLOPS = 2 * P * TOKENS * HIDDEN * CHANNELS + 2 * P * CHANNELS * CLASSES
+
+TOKEN_GROUPS = ((0, 4), (4, 4), (8, 1))
+
+UNITS = 8
+RAW_COLS = 2 * UNITS * K_PASS
+
+PIECE_COLS = 512
+FC2_PIECES = PASSES
+HEAD_PIECES = CLASSES // PIECE_COLS
+PIECES_PER_LOAD = 2
+WEIGHT_LOADS = (FC2_PIECES + HEAD_PIECES) // PIECES_PER_LOAD
+WEIGHT_BUFS = 3
+RAW_BUFS = 3
+RUN = 4
+VECTOR_COLS = 320
+POOLED_PER_ROUND = 2
+
+
+def tile_tokenmudule_pb_k_kernel(tc, hdn, fc2_w, fc2_b, head_w, head_b, out):
+    nc = tc.nc
+
+    rounds = []
+    for first_token, n_tokens in TOKEN_GROUPS:
+        for first_pass in range(0, PASSES, UNITS // n_tokens):
+            rounds.append((first_token, n_tokens, first_pass))
+    n_rounds = len(rounds)
+    n_chunks = n_rounds // 2
+    fc2_rounds = FC2_PIECES // PIECES_PER_LOAD
+
+    with ExitStack() as ctx:
+        const = ctx.enter_context(tc.tile_pool(name="const", bufs=1))
+        raw_pool = ctx.enter_context(tc.tile_pool(name="raw", bufs=RAW_BUFS))
+        wraw_pool = ctx.enter_context(tc.tile_pool(name="wraw", bufs=WEIGHT_BUFS))
+        wgrp_pool = ctx.enter_context(tc.tile_pool(name="wgrp", bufs=3))
+        hgrp_pool = ctx.enter_context(tc.tile_pool(name="hgrp", bufs=2))
+        hq_pool = ctx.enter_context(tc.tile_pool(name="hq", bufs=2))
+        x_pool = ctx.enter_context(tc.tile_pool(name="x", bufs=C_TILES))
+        work = ctx.enter_context(tc.tile_pool(name="work", bufs=2))
+        psum = ctx.enter_context(tc.psum_pool(name="psum", bufs=4))
+        ctx.enter_context(tc.manual_schedule())
+
+        w_codes = const.tile([P, FC2_PIECES, PIECE_COLS], U32, align_bytes=64)
+        w_scales = const.tile([P, FC2_PIECES, PIECE_COLS], U8, align_bytes=64)
+        hw_codes = const.tile([P, HEAD_PIECES, PIECE_COLS], U32, align_bytes=64)
+        hw_scales = const.tile([P, HEAD_PIECES, PIECE_COLS], U8, align_bytes=64)
+        head_bias = const.tile([P, CLASSES], BF16)
+        cube_sums = [const.tile([P, CHANNELS], F32, name="cube_sum%d" % i) for i in range(2)]
+
+        ident = const.tile([P, P], F32)
+        make_identity(nc, ident[:])
+
+        one = const.tile([P, 1], F32)
+        nc.vector.memset(one[:], 1.0)
+        warm_ln = const.tile([P, 1], F32)
+        nc.scalar.activation(out=warm_ln[:], in_=one[:], func=ACT.Ln)
+
+        bias_rows = const.tile([P, P], BF16)
+        nc.vector.memset(bias_rows[:], 0.0)
+        nc.sync.dma_start(out=bias_rows[0:C_TILES, :], in_=fc2_b.rearrange("(j p) -> j p", p=P))
+        bias_rows32 = const.tile([P, P], F32)
+        nc.vector.tensor_copy(out=bias_rows32[:], in_=bias_rows[:])
+        tok_bias = const.tile([P, C_TILES], F32)
+
+        def transpose_bias():
+            bias_t = psum.tile([P, P], F32, tag="xt")
+            nc.tensor.transpose(bias_t[:], bias_rows32[:], ident[:])
+            nc.vector.tensor_copy(out=tok_bias[:], in_=bias_t[:, 0:C_TILES])
+
+        raw_of = {}
+        wraw_of = {}
+
+        def load_hidden(chunk):
+            first_token, n_tokens, first_pass = rounds[2 * chunk]
+            span = RAW_COLS // n_tokens
+            k0 = first_pass * K_PASS
+            raw = raw_pool.tile([P, RAW_COLS], BF16, tag="raw")
+            for i in range(n_tokens):
+                nc.sync.dma_start(
+                    out=raw[:, i * span : (i + 1) * span],
+                    in_=hdn[:, first_token + i, k0 : k0 + span],
+                )
+            raw_of[chunk] = raw
+
+        def load_weights(load):
+            wraw = wraw_pool.tile([P, PIECES_PER_LOAD * PACK * PIECE_COLS], BF16, tag="wraw")
+            if load < fc2_rounds:
+                rows = fc2_w[load * 2 * K_PASS : (load + 1) * 2 * K_PASS, :]
+                nc.sync.dma_start(
+                    out=wraw[:].rearrange("q (s x) -> q s x", s=4),
+                    in_=rows.rearrange("(s q e) c -> q s (e c)", s=4, q=P, e=2),
+                )
+            else:
+                c0 = (load - fc2_rounds) * PIECES_PER_LOAD * PIECE_COLS
+                cols = head_w[:, c0 : c0 + PIECES_PER_LOAD * PIECE_COLS]
+                nc.sync.dma_start(
+                    out=wraw[:].rearrange("p (j n) -> p j n", j=PACK),
+                    in_=cols.rearrange("(j p) n -> p j n", p=P),
+                )
+            wraw_of[load] = wraw
+
+        wgrouped_of = {}
+
+        def regroup_piece(piece):
+            load, half = divmod(piece, PIECES_PER_LOAD)
+            wraw = wraw_of[load]
+            if piece < FC2_PIECES:
+                src = wraw[:, half * PACK * PIECE_COLS : (half + 1) * PACK * PIECE_COLS].rearrange(
+                    "p (t c) -> p t c", t=PACK
+                )
+            else:
+                src = wraw[:].rearrange("p (t n) -> p t n", t=PACK)[
+                    :, :, half * PIECE_COLS : (half + 1) * PIECE_COLS
+                ]
+            wgrouped = wgrp_pool.tile([P, PIECE_COLS, PACK], BF16, tag="wgrouped", align_bytes=64)
+            src_runs = src.rearrange("p t (c i) -> p c t i", i=RUN)
+            dst_runs = wgrouped[:].rearrange("p (c i) t -> p c t i", i=RUN)
+            split = VECTOR_COLS // RUN
+            nc.vector.tensor_copy(out=dst_runs[:, 0:split, :, :], in_=src_runs[:, 0:split, :, :])
+            nc.scalar.copy(out=dst_runs[:, split:, :, :], in_=src_runs[:, split:, :, :])
+            wgrouped_of[piece] = wgrouped
+            if half == PIECES_PER_LOAD - 1 and load + WEIGHT_BUFS < WEIGHT_LOADS:
+                load_weights(load + WEIGHT_BUFS)
+
+        def quantise_piece(piece):
+            if piece < FC2_PIECES:
+                codes, scales = w_codes[:, piece, :], w_scales[:, piece, :]
+            else:
+                codes, scales = hw_codes[:, piece - FC2_PIECES, :], hw_scales[:, piece - FC2_PIECES, :]
+            nc.vector.quantize_mx(
+                out=codes.bitcast(FP8X4),
+                scales=scales,
+                in_=wgrouped_of[piece][:].rearrange("p c t -> p (c t)"),
+            )
+
+        def pieces_before_round(r):
+            if r < fc2_rounds:
+                return (PIECES_PER_LOAD * r, PIECES_PER_LOAD * r + 1)
+            if r - fc2_rounds < HEAD_PIECES:
+                return (FC2_PIECES + r - fc2_rounds,)
+            return ()
+
+        hgrouped_of = {}
+        hq_of = {}
+
+        def transpose_round(r):
+            first_token, n_tokens, first_pass = rounds[r]
+            raw_words = raw_of[r // 2][:].bitcast(F32)
+            words_per_token = RAW_COLS // 2 // n_tokens
+            pass_in_chunk = first_pass - rounds[2 * (r // 2)][2]
+            hgrouped = hgrp_pool.tile([P, UNITS * K_PASS], BF16, tag="hgrouped", align_bytes=64)
+            grouped_words = hgrouped[:].bitcast(F32).rearrange("p (n b u) -> p n b u", n=UNITS, u=2)
+            for pair in range(UNITS // 2):
+                xt = psum.tile([P, 2, 2, P], F32, tag="xt")
+                for a in range(2):
+                    local_pass, i = divmod(2 * pair + a, n_tokens)
+                    col = i * words_per_token + (pass_in_chunk + local_pass) * (K_PASS // 2)
+                    for u in range(2):
+                        nc.tensor.transpose(
+                            xt[:, a, u, :], raw_words[:, col + u * P : col + (u + 1) * P], ident[:]
+                        )
+                nc.scalar.copy(
+                    out=grouped_words[:, 2 * pair : 2 * pair + 2, :, :],
+                    in_=xt[:].rearrange("p a u b -> p a b u"),
+                )
+            hgrouped_of[r] = hgrouped
+
+        def quantise_round(r):
+            hcodes = hq_pool.tile([P, UNITS * P], U32, tag="hcodes", align_bytes=64)
+            hscales = hq_pool.tile([P, UNITS * P], U8, tag="hscales", align_bytes=64)
+            nc.vector.quantize_mx(out=hcodes[:].bitcast(FP8X4), scales=hscales[:], in_=hgrouped_of[r][:])
+            hq_of[r] = (hcodes, hscales)
+
+        acc = {}
+
+        def multiply_round(r):
+            first_token, n_tokens, first_pass = rounds[r]
+            n_cols = n_tokens * P
+            hcodes, hscales = hq_of[r]
+            if first_pass == 0:
+                for j in range(C_TILES):
+                    acc[j] = psum.tile([P, n_cols], F32, tag="acc", name="acc%d" % j)
+            for j in range(C_TILES):
+                for local_pass in range(UNITS // n_tokens):
+                    g = first_pass + local_pass
+                    nc.tensor.matmul_mx(
+                        out=acc[j][:],
+                        lhsT=w_codes[:, g, j * P : (j + 1) * P].bitcast(FP8X4),
+                        lhsT_scale=w_scales[:, g, j * P : (j + 1) * P],
+                        rhs=hcodes[:, local_pass * n_cols : (local_pass + 1) * n_cols].bitcast(FP8X4),
+                        rhs_scale=hscales[:, local_pass * n_cols : (local_pass + 1) * n_cols],
+                        start=(g == 0),
+                        stop=(g == PASSES - 1),
+                    )
+
+        def clamp(j, x):
+            nc.vector.tensor_scalar(
+                out=x, in0=acc[j][:], scalar1=tok_bias[:, j : j + 1], scalar2=EPS_GEM, op0=ALU.add, op1=ALU.max
+            )
+
+        def cube(x):
+            x2 = work.tile([P, BANK], F32, tag="x2")
+            nc.scalar.activation(out=x2[:], in_=x[:], func=ACT.Square)
+            x3 = work.tile([P, BANK], F32, tag="x3")
+            nc.vector.tensor_tensor(out=x3[:], in0=x2[:], in1=x[:], op=ALU.mult)
+            return x3
+
+        def pool_bank(x, n_tokens, dest):
+            x3 = cube(x)
+            nc.vector.tensor_reduce(
+                out=dest, in_=x3[:].rearrange("p (i b) -> p b i", i=n_tokens), axis=AX.X, op=ALU.add
+            )
+
+        load_weights(0)
+        load_hidden(0)
+        load_weights(1)
+        load_weights(2)
+        load_hidden(1)
+        for piece in pieces_before_round(0):
+            regroup_piece(piece)
+        for piece in pieces_before_round(0):
+            quantise_piece(piece)
+
+        group = 0
+        clamped = []
+        closed_at = 0
+        for r in range(n_rounds):
+            transpose_round(r)
+            if r == 0:
+                transpose_bias()
+            new_pieces = pieces_before_round(r + 1)
+            for piece in new_pieces:
+                regroup_piece(piece)
+            if r % 2 == 0 and r // 2 + 2 < n_chunks:
+                load_hidden(r // 2 + 2)
+                if r // 2 + 2 == n_chunks - 1:
+                    nc.sync.dma_start(out=head_bias[:], in_=head_b.partition_broadcast(P))
+            if r >= 1:
+                multiply_round(r - 1)
+            quantise_round(r)
+            if r >= 1 and rounds[r][2] == 0:
+                clamped = []
+                closed_at = r
+                for j in range(C_TILES):
+                    x = x_pool.tile([P, BANK], F32, tag="x")
+                    clamp(j, x[:])
+                    clamped.append(x)
+                group += 1
+            for piece in new_pieces:
+                quantise_piece(piece)
+            first = POOLED_PER_ROUND * (r - closed_at)
+            for j in range(first, min(first + POOLED_PER_ROUND, len(clamped))):
+                pool_bank(clamped[j], rounds[closed_at - 1][1], cube_sums[group - 1][:, j * P : (j + 1) * P])
+
+        multiply_round(n_rounds - 1)
+        both = const.tile([P, CHANNELS], F32)
+        nc.vector.tensor_tensor(out=both[:], in0=cube_sums[0][:], in1=cube_sums[1][:], op=ALU.add)
+        x = x_pool.tile([P, BANK], F32, tag="x")
+        for j in range(C_TILES):
+            clamp(j, x[:, j * P : (j + 1) * P])
+        x3 = cube(x)
+        total = const.tile([P, CHANNELS], F32)
+        nc.vector.tensor_tensor(out=total[:], in0=x3[:], in1=both[:], op=ALU.add)
+        log_mean = const.tile([P, CHANNELS], F32)
+        nc.scalar.activation(out=log_mean[:], in_=total[:], func=ACT.Ln, scale=1.0 / TOKENS)
+        g_grouped = const.tile([P, P, PACK], BF16, align_bytes=64)
+        nc.scalar.activation(
+            out=g_grouped[:],
+            in_=log_mean[:].rearrange("p (j b) -> p b j", j=PACK),
+            func=ACT.Exp,
+            scale=1.0 / 3.0,
+        )
+        warm_sqrt = const.tile([P, 1], F32)
+        nc.scalar.activation(out=warm_sqrt[:], in_=one[:], func=ACT.Sqrt)
+        g_codes = const.tile([P, P], U32, align_bytes=64)
+        g_scales = const.tile([P, P], U8, align_bytes=64)
+        nc.vector.quantize_mx(
+            out=g_codes[:].bitcast(FP8X4), scales=g_scales[:], in_=g_grouped[:].rearrange("p b j -> p (b j)")
+        )
+
+        d = const.tile([P, CLASSES], F32)
+        squares = const.tile([P, D_BANKS], F32)
+        for n in range(D_BANKS):
+            cols = slice(n * BANK, (n + 1) * BANK)
+            d_bank = psum.tile([P, BANK], F32, tag=("acc" if n < 4 else "xt"), name="d_bank")
+            nc.tensor.matmul_mx(
+                out=d_bank[:],
+                lhsT=g_codes[:].bitcast(FP8X4),
+                lhsT_scale=g_scales[:],
+                rhs=hw_codes[:, n, :].bitcast(FP8X4),
+                rhs_scale=hw_scales[:, n, :],
+                start=True,
+                stop=True,
+            )
+            nc.vector.tensor_tensor(out=d[:, cols], in0=d_bank[:], in1=head_bias[:, cols], op=ALU.add)
+            d2 = work.tile([P, BANK], F32, tag="x2")
+            nc.scalar.activation(out=d2[:], in_=d[:, cols], func=ACT.Square, accum_out=squares[:, n : n + 1])
+        norm = const.tile([P, 1], F32)
+        nc.vector.tensor_reduce(out=norm[:], in_=squares[:], axis=AX.X, op=ALU.add)
+        nc.scalar.activation(out=norm[:], in_=norm[:], func=ACT.Sqrt)
+        nc.vector.tensor_scalar(out=norm[:], in0=norm[:], scalar1=EPS_NORM, scalar2=None, op0=ALU.max)
+        inv_norm = const.tile([P, 1], F32)
+        nc.vector.reciprocal(out=inv_norm[:], in_=norm[:])
+        for n in range(D_BANKS):
+            cols = slice(n * BANK, (n + 1) * BANK)
+            if n % 2 == 0:
+                nc.vector.tensor_scalar(
+                    out=d[:, cols], in0=d[:, cols], scalar1=inv_norm[:], scalar2=None, op0=ALU.mult
+                )
+            else:
+                nc.scalar.activation(out=d[:, cols], in_=d[:, cols], func=ACT.Copy, scale=inv_norm[:])
+                both_cols = slice((n - 1) * BANK, (n + 1) * BANK)
+                nc.sync.dma_start(out=out[:, both_cols], in_=d[:, both_cols])

@@ -44,6 +44,8 @@ RAW_BUFS = 3
 RUN = 4
 VECTOR_COLS = 320
 POOLED_PER_ROUND = 2
+HEAD_FIRST_ROUND = 12
+FIRST_CHUNK_BEFORE_HEAD = 5
 
 
 def tile_tokenmudule_pb_k_kernel(tc, hdn, fc2_w, fc2_b, head_w, head_b, out):
@@ -148,7 +150,7 @@ def tile_tokenmudule_pb_k_kernel(tc, hdn, fc2_w, fc2_b, head_w, head_b, out):
             nc.vector.tensor_copy(out=dst_runs[:, 0:split, :, :], in_=src_runs[:, 0:split, :, :])
             nc.scalar.copy(out=dst_runs[:, split:, :, :], in_=src_runs[:, split:, :, :])
             wgrouped_of[piece] = wgrouped
-            if half == PIECES_PER_LOAD - 1 and load + WEIGHT_BUFS < WEIGHT_LOADS:
+            if half == PIECES_PER_LOAD - 1 and load + WEIGHT_BUFS < fc2_rounds:
                 load_weights(load + WEIGHT_BUFS)
 
         def quantise_piece(piece):
@@ -165,8 +167,9 @@ def tile_tokenmudule_pb_k_kernel(tc, hdn, fc2_w, fc2_b, head_w, head_b, out):
         def pieces_before_round(r):
             if r < fc2_rounds:
                 return (PIECES_PER_LOAD * r, PIECES_PER_LOAD * r + 1)
-            if r - fc2_rounds < HEAD_PIECES:
-                return (FC2_PIECES + r - fc2_rounds,)
+            if 0 <= r - HEAD_FIRST_ROUND < HEAD_PIECES // PIECES_PER_LOAD:
+                first = FC2_PIECES + PIECES_PER_LOAD * (r - HEAD_FIRST_ROUND)
+                return (first, first + 1)
             return ()
 
         hgrouped_of = {}
@@ -253,17 +256,15 @@ def tile_tokenmudule_pb_k_kernel(tc, hdn, fc2_w, fc2_b, head_w, head_b, out):
         group = 0
         clamped = []
         closed_at = 0
+
+        def pool_banks(first):
+            for j in range(max(first, 0), min(first + POOLED_PER_ROUND, len(clamped))):
+                pool_bank(clamped[j], rounds[closed_at - 1][1], cube_sums[group - 1][:, j * P : (j + 1) * P])
+
         for r in range(n_rounds):
             transpose_round(r)
             if r == 0:
                 transpose_bias()
-            new_pieces = pieces_before_round(r + 1)
-            for piece in new_pieces:
-                regroup_piece(piece)
-            if r % 2 == 0 and r // 2 + 2 < n_chunks:
-                load_hidden(r // 2 + 2)
-                if r // 2 + 2 == n_chunks - 1:
-                    nc.sync.dma_start(out=head_bias[:], in_=head_b.partition_broadcast(P))
             if r >= 1:
                 multiply_round(r - 1)
             quantise_round(r)
@@ -275,21 +276,37 @@ def tile_tokenmudule_pb_k_kernel(tc, hdn, fc2_w, fc2_b, head_w, head_b, out):
                     clamp(j, x[:])
                     clamped.append(x)
                 group += 1
+            new_pieces = pieces_before_round(r + 1)
+            for piece in new_pieces:
+                regroup_piece(piece)
+            pool_banks(POOLED_PER_ROUND * (r - closed_at - 1))
             for piece in new_pieces:
                 quantise_piece(piece)
-            first = POOLED_PER_ROUND * (r - closed_at)
-            for j in range(first, min(first + POOLED_PER_ROUND, len(clamped))):
-                pool_bank(clamped[j], rounds[closed_at - 1][1], cube_sums[group - 1][:, j * P : (j + 1) * P])
+            if r % 2 == 0 and r // 2 + 2 < n_chunks:
+                chunk = r // 2 + 2
+                load_hidden(chunk)
+                if chunk >= FIRST_CHUNK_BEFORE_HEAD:
+                    load_weights(fc2_rounds + chunk - FIRST_CHUNK_BEFORE_HEAD)
+                if chunk == n_chunks - 1:
+                    nc.sync.dma_start(out=head_bias[:], in_=head_b.partition_broadcast(P))
 
         multiply_round(n_rounds - 1)
+        pool_banks(POOLED_PER_ROUND * (n_rounds - closed_at - 1))
         both = const.tile([P, CHANNELS], F32)
         nc.vector.tensor_tensor(out=both[:], in0=cube_sums[0][:], in1=cube_sums[1][:], op=ALU.add)
         x = x_pool.tile([P, BANK], F32, tag="x")
-        for j in range(C_TILES):
-            clamp(j, x[:, j * P : (j + 1) * P])
-        x3 = cube(x)
+        x2 = work.tile([P, BANK], F32, tag="x2")
+        x3 = work.tile([P, BANK], F32, tag="x3")
         total = const.tile([P, CHANNELS], F32)
-        nc.vector.tensor_tensor(out=total[:], in0=x3[:], in1=both[:], op=ALU.add)
+        for j in range(C_TILES + 1):
+            if j < C_TILES:
+                cols = slice(j * P, (j + 1) * P)
+                clamp(j, x[:, cols])
+                nc.scalar.activation(out=x2[:, cols], in_=x[:, cols], func=ACT.Square)
+            if j >= 1:
+                cols = slice((j - 1) * P, j * P)
+                nc.vector.tensor_tensor(out=x3[:, cols], in0=x2[:, cols], in1=x[:, cols], op=ALU.mult)
+                nc.vector.tensor_tensor(out=total[:, cols], in0=x3[:, cols], in1=both[:, cols], op=ALU.add)
         log_mean = const.tile([P, CHANNELS], F32)
         nc.scalar.activation(out=log_mean[:], in_=total[:], func=ACT.Ln, scale=1.0 / TOKENS)
         g_grouped = const.tile([P, P, PACK], BF16, align_bytes=64)

from contextlib import ExitStack

import concourse.mybir as mybir
from concourse.masks import make_identity

F32 = mybir.dt.float32
BF16 = mybir.dt.bfloat16
U32 = mybir.dt.uint32
U8 = mybir.dt.uint8
FP8X4 = mybir.dt.float8_e4m3fn_x4
ALU = mybir.AluOpType
ACT = mybir.ActivationFunctionType
AX = mybir.AxisListType

P = 128
PACK = 4
K_PASS = P * PACK
TOKENS = 9
HIDDEN = 8192
CHANNELS = 512
CLASSES = 4096
PASSES = HIDDEN // K_PASS
C_TILES = CHANNELS // P
BANK = 512
D_BANKS = CLASSES // BANK

EPS_GEM = 1e-6
EPS_NORM = 1e-12

FLOPS = 2 * P * TOKENS * HIDDEN * CHANNELS + 2 * P * CHANNELS * CLASSES

TOKEN_GROUPS = ((0, 4), (4, 4), (8, 1))

UNITS = 8
RAW_COLS = 2 * UNITS * K_PASS

PIECE_COLS = 512
FC2_PIECES = PASSES
HEAD_PIECES = CLASSES // PIECE_COLS
PIECES_PER_LOAD = 2
WEIGHT_LOADS = (FC2_PIECES + HEAD_PIECES) // PIECES_PER_LOAD
WEIGHT_BUFS = 3
RAW_BUFS = 3
RUN = 4
VECTOR_COLS = 320
POOLED_PER_ROUND = 2
HEAD_FIRST_ROUND = 12
FIRST_CHUNK_BEFORE_HEAD = 5


def tile_tokenmudule_pb_k_kernel(tc, hdn, fc2_w, fc2_b, head_w, head_b, out):
    nc = tc.nc

    rounds = []
    for first_token, n_tokens in TOKEN_GROUPS:
        for first_pass in range(0, PASSES, UNITS // n_tokens):
            rounds.append((first_token, n_tokens, first_pass))
    n_rounds = len(rounds)
    n_chunks = n_rounds // 2
    fc2_rounds = FC2_PIECES // PIECES_PER_LOAD

    with ExitStack() as ctx:
        const = ctx.enter_context(tc.tile_pool(name="const", bufs=1))
        raw_pool = ctx.enter_context(tc.tile_pool(name="raw", bufs=RAW_BUFS))
        wraw_pool = ctx.enter_context(tc.tile_pool(name="wraw", bufs=WEIGHT_BUFS))
        wgrp_pool = ctx.enter_context(tc.tile_pool(name="wgrp", bufs=3))
        hgrp_pool = ctx.enter_context(tc.tile_pool(name="hgrp", bufs=2))
        hq_pool = ctx.enter_context(tc.tile_pool(name="hq", bufs=2))
        x_pool = ctx.enter_context(tc.tile_pool(name="x", bufs=C_TILES))
        work = ctx.enter_context(tc.tile_pool(name="work", bufs=2))
        psum = ctx.enter_context(tc.psum_pool(name="psum", bufs=4))
        ctx.enter_context(tc.manual_schedule())

        w_codes = const.tile([P, FC2_PIECES, PIECE_COLS], U32, align_bytes=64)
        w_scales = const.tile([P, FC2_PIECES, PIECE_COLS], U8, align_bytes=64)
        hw_codes = const.tile([P, HEAD_PIECES, PIECE_COLS], U32, align_bytes=64)
        hw_scales = const.tile([P, HEAD_PIECES, PIECE_COLS], U8, align_bytes=64)
        head_bias = const.tile([P, CLASSES], BF16)
        cube_sums = [const.tile([P, CHANNELS], F32, name="cube_sum%d" % i) for i in range(2)]

        ident = const.tile([P, P], F32)
        make_identity(nc, ident[:])

        one = const.tile([P, 1], F32)
        nc.vector.memset(one[:], 1.0)
        warm_ln = const.tile([P, 1], F32)
        nc.scalar.activation(out=warm_ln[:], in_=one[:], func=ACT.Ln)

        bias_rows = const.tile([P, P], BF16)
        nc.vector.memset(bias_rows[:], 0.0)
        nc.sync.dma_start(out=bias_rows[0:C_TILES, :], in_=fc2_b.rearrange("(j p) -> j p", p=P))
        bias_rows32 = const.tile([P, P], F32)
        nc.vector.tensor_copy(out=bias_rows32[:], in_=bias_rows[:])
        tok_bias = const.tile([P, C_TILES], F32)

        def transpose_bias():
            bias_t = psum.tile([P, P], F32, tag="xt")
            nc.tensor.transpose(bias_t[:], bias_rows32[:], ident[:])
            nc.vector.tensor_copy(out=tok_bias[:], in_=bias_t[:, 0:C_TILES])

        raw_of = {}
        wraw_of = {}

        def load_hidden(chunk):
            first_token, n_tokens, first_pass = rounds[2 * chunk]
            span = RAW_COLS // n_tokens
            k0 = first_pass * K_PASS
            raw = raw_pool.tile([P, RAW_COLS], BF16, tag="raw")
            for i in range(n_tokens):
                nc.sync.dma_start(
                    out=raw[:, i * span : (i + 1) * span],
                    in_=hdn[:, first_token + i, k0 : k0 + span],
                )
            raw_of[chunk] = raw

        def load_weights(load):
            wraw = wraw_pool.tile([P, PIECES_PER_LOAD * PACK * PIECE_COLS], BF16, tag="wraw")
            if load < fc2_rounds:
                rows = fc2_w[load * 2 * K_PASS : (load + 1) * 2 * K_PASS, :]
                nc.sync.dma_start(
                    out=wraw[:].rearrange("q (s x) -> q s x", s=4),
                    in_=rows.rearrange("(s q e) c -> q s (e c)", s=4, q=P, e=2),
                )
            else:
                c0 = (load - fc2_rounds) * PIECES_PER_LOAD * PIECE_COLS
                cols = head_w[:, c0 : c0 + PIECES_PER_LOAD * PIECE_COLS]
                nc.sync.dma_start(
                    out=wraw[:].rearrange("p (j n) -> p j n", j=PACK),
                    in_=cols.rearrange("(j p) n -> p j n", p=P),
                )
            wraw_of[load] = wraw

        wgrouped_of = {}

        def regroup_piece(piece):
            load, half = divmod(piece, PIECES_PER_LOAD)
            wraw = wraw_of[load]
            if piece < FC2_PIECES:
                src = wraw[:, half * PACK * PIECE_COLS : (half + 1) * PACK * PIECE_COLS].rearrange(
                    "p (t c) -> p t c", t=PACK
                )
            else:
                src = wraw[:].rearrange("p (t n) -> p t n", t=PACK)[
                    :, :, half * PIECE_COLS : (half + 1) * PIECE_COLS
                ]
            wgrouped = wgrp_pool.tile([P, PIECE_COLS, PACK], BF16, tag="wgrouped", align_bytes=64)
            src_runs = src.rearrange("p t (c i) -> p c t i", i=RUN)
            dst_runs = wgrouped[:].rearrange("p (c i) t -> p c t i", i=RUN)
            split = VECTOR_COLS // RUN
            nc.vector.tensor_copy(out=dst_runs[:, 0:split, :, :], in_=src_runs[:, 0:split, :, :])
            nc.scalar.copy(out=dst_runs[:, split:, :, :], in_=src_runs[:, split:, :, :])
            wgrouped_of[piece] = wgrouped
            if half == PIECES_PER_LOAD - 1 and load + WEIGHT_BUFS < fc2_rounds:
                load_weights(load + WEIGHT_BUFS)

        def quantise_piece(piece):
            if piece < FC2_PIECES:
                codes, scales = w_codes[:, piece, :], w_scales[:, piece, :]
            else:
                codes, scales = hw_codes[:, piece - FC2_PIECES, :], hw_scales[:, piece - FC2_PIECES, :]
            nc.vector.quantize_mx(
                out=codes.bitcast(FP8X4),
                scales=scales,
                in_=wgrouped_of[piece][:].rearrange("p c t -> p (c t)"),
            )

        def pieces_before_round(r):
            if r < fc2_rounds:
                return (PIECES_PER_LOAD * r, PIECES_PER_LOAD * r + 1)
            if 0 <= r - HEAD_FIRST_ROUND < HEAD_PIECES // PIECES_PER_LOAD:
                first = FC2_PIECES + PIECES_PER_LOAD * (r - HEAD_FIRST_ROUND)
                return (first, first + 1)
            return ()

        hgrouped_of = {}
        hq_of = {}

        def transpose_round(r):
            first_token, n_tokens, first_pass = rounds[r]
            raw_words = raw_of[r // 2][:].bitcast(F32)
            words_per_token = RAW_COLS // 2 // n_tokens
            pass_in_chunk = first_pass - rounds[2 * (r // 2)][2]
            hgrouped = hgrp_pool.tile([P, UNITS * K_PASS], BF16, tag="hgrouped", align_bytes=64)
            grouped_words = hgrouped[:].bitcast(F32).rearrange("p (n b u) -> p n b u", n=UNITS, u=2)
            for pair in range(UNITS // 2):
                xt = psum.tile([P, 2, 2, P], F32, tag="xt")
                for a in range(2):
                    local_pass, i = divmod(2 * pair + a, n_tokens)
                    col = i * words_per_token + (pass_in_chunk + local_pass) * (K_PASS // 2)
                    for u in range(2):
                        nc.tensor.transpose(
                            xt[:, a, u, :], raw_words[:, col + u * P : col + (u + 1) * P], ident[:]
                        )
                nc.scalar.copy(
                    out=grouped_words[:, 2 * pair : 2 * pair + 2, :, :],
                    in_=xt[:].rearrange("p a u b -> p a b u"),
                )
            hgrouped_of[r] = hgrouped

        def quantise_round(r):
            hcodes = hq_pool.tile([P, UNITS * P], U32, tag="hcodes", align_bytes=64)
            hscales = hq_pool.tile([P, UNITS * P], U8, tag="hscales", align_bytes=64)
            nc.vector.quantize_mx(out=hcodes[:].bitcast(FP8X4), scales=hscales[:], in_=hgrouped_of[r][:])
            hq_of[r] = (hcodes, hscales)

        acc = {}

        def multiply_round(r):
            first_token, n_tokens, first_pass = rounds[r]
            n_cols = n_tokens * P
            hcodes, hscales = hq_of[r]
            if first_pass == 0:
                for j in range(C_TILES):
                    acc[j] = psum.tile([P, n_cols], F32, tag="acc", name="acc%d" % j)
            for j in range(C_TILES):
                for local_pass in range(UNITS // n_tokens):
                    g = first_pass + local_pass
                    nc.tensor.matmul_mx(
                        out=acc[j][:],
                        lhsT=w_codes[:, g, j * P : (j + 1) * P].bitcast(FP8X4),
                        lhsT_scale=w_scales[:, g, j * P : (j + 1) * P],
                        rhs=hcodes[:, local_pass * n_cols : (local_pass + 1) * n_cols].bitcast(FP8X4),
                        rhs_scale=hscales[:, local_pass * n_cols : (local_pass + 1) * n_cols],
                        start=(g == 0),
                        stop=(g == PASSES - 1),
                    )

        def clamp(j, x):
            nc.vector.tensor_scalar(
                out=x, in0=acc[j][:], scalar1=tok_bias[:, j : j + 1], scalar2=EPS_GEM, op0=ALU.add, op1=ALU.max
            )

        def cube(x):
            x2 = work.tile([P, BANK], F32, tag="x2")
            nc.scalar.activation(out=x2[:], in_=x[:], func=ACT.Square)
            x3 = work.tile([P, BANK], F32, tag="x3")
            nc.vector.tensor_tensor(out=x3[:], in0=x2[:], in1=x[:], op=ALU.mult)
            return x3

        def pool_bank(x, n_tokens, dest):
            x3 = cube(x)
            nc.vector.tensor_reduce(
                out=dest, in_=x3[:].rearrange("p (i b) -> p b i", i=n_tokens), axis=AX.X, op=ALU.add
            )

        load_weights(0)
        load_hidden(0)
        load_weights(1)
        load_weights(2)
        load_hidden(1)
        for piece in pieces_before_round(0):
            regroup_piece(piece)
        for piece in pieces_before_round(0):
            quantise_piece(piece)

        group = 0
        clamped = []
        closed_at = 0

        def pool_banks(first):
            for j in range(max(first, 0), min(first + POOLED_PER_ROUND, len(clamped))):
                pool_bank(clamped[j], rounds[closed_at - 1][1], cube_sums[group - 1][:, j * P : (j + 1) * P])

        for r in range(n_rounds):
            transpose_round(r)
            if r == 0:
                transpose_bias()
            if r >= 1:
                multiply_round(r - 1)
            quantise_round(r)
            if r >= 1 and rounds[r][2] == 0:
                clamped = []
                closed_at = r
                for j in range(C_TILES):
                    x = x_pool.tile([P, BANK], F32, tag="x")
                    clamp(j, x[:])
                    clamped.append(x)
                group += 1
            new_pieces = pieces_before_round(r + 1)
            for piece in new_pieces:
                regroup_piece(piece)
            pool_banks(POOLED_PER_ROUND * (r - closed_at - 1))
            for piece in new_pieces:
                quantise_piece(piece)
            if r % 2 == 0 and r // 2 + 2 < n_chunks:
                chunk = r // 2 + 2
                load_hidden(chunk)
                if chunk >= FIRST_CHUNK_BEFORE_HEAD:
                    load_weights(fc2_rounds + chunk - FIRST_CHUNK_BEFORE_HEAD)
                if chunk == n_chunks - 1:
                    nc.sync.dma_start(out=head_bias[:], in_=head_b.partition_broadcast(P))

        multiply_round(n_rounds - 1)
        pool_banks(POOLED_PER_ROUND * (n_rounds - closed_at - 1))
        both = const.tile([P, CHANNELS], F32)
        nc.vector.tensor_tensor(out=both[:], in0=cube_sums[0][:], in1=cube_sums[1][:], op=ALU.add)
        x = x_pool.tile([P, BANK], F32, tag="x")
        x2 = work.tile([P, BANK], F32, tag="x2")
        x3 = work.tile([P, BANK], F32, tag="x3")
        total = const.tile([P, CHANNELS], F32)
        for j in range(C_TILES + 1):
            if j < C_TILES:
                cols = slice(j * P, (j + 1) * P)
                clamp(j, x[:, cols])
                nc.scalar.activation(out=x2[:, cols], in_=x[:, cols], func=ACT.Square)
            if j >= 1:
                cols = slice((j - 1) * P, j * P)
                nc.vector.tensor_tensor(out=x3[:, cols], in0=x2[:, cols], in1=x[:, cols], op=ALU.mult)
                nc.vector.tensor_tensor(out=total[:, cols], in0=x3[:, cols], in1=both[:, cols], op=ALU.add)
        log_mean = const.tile([P, CHANNELS], F32)
        nc.scalar.activation(out=log_mean[:], in_=total[:], func=ACT.Ln, scale=1.0 / TOKENS)
        g_grouped = const.tile([P, P, PACK], BF16, align_bytes=64)
        nc.scalar.activation(
            out=g_grouped[:],
            in_=log_mean[:].rearrange("p (j b) -> p b j", j=PACK),
            func=ACT.Exp,
            scale=1.0 / 3.0,
        )
        warm_sqrt = const.tile([P, 1], F32)
        nc.scalar.activation(out=warm_sqrt[:], in_=one[:], func=ACT.Sqrt)
        g_codes = const.tile([P, P], U32, align_bytes=64)
        g_scales = const.tile([P, P], U8, align_bytes=64)
        nc.vector.quantize_mx(
            out=g_codes[:].bitcast(FP8X4), scales=g_scales[:], in_=g_grouped[:].rearrange("p b j -> p (b j)")
        )

        d = const.tile([P, CLASSES], F32)
        squares = const.tile([P, D_BANKS], F32)
        for n in range(D_BANKS):
            cols = slice(n * BANK, (n + 1) * BANK)
            d_bank = psum.tile([P, BANK], F32, tag=("acc" if n < 4 else "xt"), name="d_bank")
            nc.tensor.matmul_mx(
                out=d_bank[:],
                lhsT=g_codes[:].bitcast(FP8X4),
                lhsT_scale=g_scales[:],
                rhs=hw_codes[:, n, :].bitcast(FP8X4),
                rhs_scale=hw_scales[:, n, :],
                start=True,
                stop=True,
            )
            nc.vector.tensor_tensor(out=d[:, cols], in0=d_bank[:], in1=head_bias[:, cols], op=ALU.add)
            d2 = work.tile([P, BANK], F32, tag="x2")
            nc.scalar.activation(out=d2[:], in_=d[:, cols], func=ACT.Square, accum_out=squares[:, n : n + 1])
        norm = const.tile([P, 1], F32)
        nc.vector.tensor_reduce(out=norm[:], in_=squares[:], axis=AX.X, op=ALU.add)
        nc.scalar.activation(out=norm[:], in_=norm[:], func=ACT.Sqrt)
        nc.vector.tensor_scalar(out=norm[:], in0=norm[:], scalar1=EPS_NORM, scalar2=None, op0=ALU.max)
        inv_norm = const.tile([P, 1], F32)
        nc.vector.reciprocal(out=inv_norm[:], in_=norm[:])
        for n in range(D_BANKS):
            cols = slice(n * BANK, (n + 1) * BANK)
            if n % 2 == 0:
                nc.vector.tensor_scalar(
                    out=d[:, cols], in0=d[:, cols], scalar1=inv_norm[:], scalar2=None, op0=ALU.mult
                )
            else:
                nc.scalar.activation(out=d[:, cols], in_=d[:, cols], func=ACT.Copy, scale=inv_norm[:])
                both_cols = slice((n - 1) * BANK, (n + 1) * BANK)
                nc.sync.dma_start(out=out[:, both_cols], in_=d[:, both_cols])
